import numpy as np
import ml_dtypes

BF16 = ml_dtypes.bfloat16


def bf(x):
    return np.asarray(x, np.float32).astype(BF16)


def f32(x):
    return np.asarray(x, np.float32)


def f64(x):
    return np.asarray(x).astype(np.float64)


def striped(idx):
    return np.tile(idx.reshape(-1, 16).T, (8, 1))


C, S, K, N, T = 512, 256, 4, 1024, 512
LEVELS, ZERO = 16, 8


def setup_inputs():
    return {"scales": f32(0.05 + 0.1 * np.random.uniform(size=(C, S))), "wq": f32(np.random.choice(LEVELS, (C, N))), "act": bf(0.25 * np.random.standard_normal((N, T))), "bias": f32(np.random.standard_normal((C, 1))), "offs": striped(np.concatenate([np.random.permutation(S) for _ in range(K)]))}


def reference(scales, wq, act, bias, offs):
    idx = offs[:16].T.reshape(-1)
    w = f64(scales)[:, idx] * (f64(wq) - ZERO)
    return w @ f64(act) + f64(bias)

@@ -1,0 +1,99 @@
+import concourse.mybir as mybir
+from concourse.masks import make_identity
+
+F32, BF16, U16 = mybir.dt.float32, mybir.dt.bfloat16, mybir.dt.uint16
+MULT = mybir.AluOpType.mult
+COPY = mybir.ActivationFunctionType.Copy
+IDENTITY = mybir.ActivationFunctionType.Identity
+
+P = 128
+C, S, N, T = 512, 256, 1024, 512
+ZERO_POINT = 8.0
+BLOCKS = C // P
+PIECE = S
+PIECES = N // PIECE
+FLIPS = PIECE // P
+AHEAD = 2
+
+FLOPS = 2 * C * N * T
+
+
+def tile_autograd4bitquantlinear_kernel(tc, scales, wq, act, bias, offs, out):
+    nc = tc.nc
+    act_rows = act.rearrange("(k p) t -> p k t", p=P)
+
+    with (
+        tc.tile_pool(name="held", bufs=1) as held,
+        tc.tile_pool(name="ring", bufs=3) as ring,
+        tc.tile_pool(name="flipped", bufs=2) as flipped,
+        tc.psum_pool(name="flip_banks", bufs=3) as flip_banks,
+        tc.psum_pool(name="sum_banks", bufs=2) as sum_banks,
+    ):
+        identity = held.tile([P, P], F32, name="identity")
+        make_identity(nc, identity[:])
+
+        offsets = held.tile([P, N // 16], U16, name="offsets")
+        nc.sync.dma_start(offsets[:], offs)
+        scale_tiles = [held.tile([P, S], F32, name=f"scales{b}") for b in range(BLOCKS)]
+        code_tiles = [held.tile([P, N], F32, name=f"codes{b}") for b in range(BLOCKS)]
+        bias_tiles = [held.tile([P, 1], F32, name=f"bias{b}") for b in range(BLOCKS)]
+        act_tile = held.tile([P, N // P, T], BF16, name="act_tile")
+        for b in range(BLOCKS):
+            rows = slice(b * P, (b + 1) * P)
+            nc.sync.dma_start(scale_tiles[b][:], scales[rows, :])
+            for r in range(PIECES):
+                cols = slice(r * PIECE, (r + 1) * PIECE)
+                nc.sync.dma_start(code_tiles[b][:, cols], wq[rows, cols])
+                if b == 0:
+                    ks = slice(r * FLIPS, (r + 1) * FLIPS)
+                    nc.sync.dma_start(act_tile[:, ks, :], act_rows[:, ks, :])
+            nc.sync.dma_start(bias_tiles[b][:], bias[rows, :])
+
+        centred_tiles = [held.tile([P, N], F32, name=f"centred{b}") for b in range(BLOCKS)]
+        steps = [(b, r) for b in range(BLOCKS) for r in range(PIECES)]
+        weights = {}
+        sums = {}
+
+        def centre(b, r):
+            cols = slice(r * PIECE, (r + 1) * PIECE)
+            nc.scalar.activation(centred_tiles[b][:, cols], code_tiles[b][:, cols], COPY, bias=-ZERO_POINT)
+
+        def dequantise_and_flip(b, r):
+            cols = slice(r * PIECE, (r + 1) * PIECE)
+            picked = scale_tiles[b][:].indirect(offsets[:, r * (PIECE // 16) : (r + 1) * (PIECE // 16)])
+            w_piece = ring.tile([P, PIECE], F32, name="w_piece")
+            nc.vector.tensor_tensor(w_piece[:], picked, centred_tiles[b][:, cols], MULT)
+            bank = flip_banks.tile([P, PIECE], F32, name="bank")
+            for f in range(FLIPS):
+                part = slice(f * P, (f + 1) * P)
+                nc.tensor.transpose(bank[:, part], w_piece[:, part], identity[:])
+            if r == 0:
+                weights[b] = flipped.tile([P, N], BF16, name="weights")
+            nc.scalar.activation(weights[b][:, cols], bank[:], COPY)
+
+        def multiply(b, r):
+            if r == 0:
+                sums[b] = sum_banks.tile([P, T], F32, name="sums")
+            for f in range(FLIPS):
+                k = r * FLIPS + f
+                nc.tensor.matmul(
+                    sums[b][:],
+                    weights[b][:, k * P : (k + 1) * P],
+                    act_tile[:, k, :],
+                    start=(k == 0),
+                    stop=(k == N // P - 1),
+                )
+            if r == PIECES - 1:
+                result = ring.tile([P, T], F32, name="result")
+                nc.scalar.activation(result[:], sums[b][:], IDENTITY, bias=bias_tiles[b][:])
+                nc.sync.dma_start(out[b * P : (b + 1) * P, :], result[:])
+
+        for i in range(AHEAD):
+            centre(*steps[i])
+        for i in range(len(steps) + 1):
+            if i + AHEAD < len(steps):
+                centre(*steps[i + AHEAD])
+            if i < len(steps):
+                dequantise_and_flip(*steps[i])
+            if i >= 1:
+                multiply(*steps[i - 1])

@@ -2,7 +2,7 @@ import concourse.mybir as mybir
 from concourse.masks import make_identity
 
 F32, BF16, U16 = mybir.dt.float32, mybir.dt.bfloat16, mybir.dt.uint16
-MULT = mybir.AluOpType.mult
+MULT, ADD = mybir.AluOpType.mult, mybir.AluOpType.add
 COPY = mybir.ActivationFunctionType.Copy
 IDENTITY = mybir.ActivationFunctionType.Identity
 
@@ -13,7 +13,8 @@ BLOCKS = C // P
 PIECE = S
 PIECES = N // PIECE
 FLIPS = PIECE // P
-AHEAD = 2
+WARM = 6
+LAG = 2
 
 FLOPS = 2 * C * N * T
 
@@ -24,19 +25,29 @@ def tile_autograd4bitquantlinear_kernel(tc, scales, wq, act, bias, offs, out):
 
     with (
         tc.tile_pool(name="held", bufs=1) as held,
-        tc.tile_pool(name="ring", bufs=3) as ring,
+        tc.tile_pool(name="ring", bufs=LAG + 2) as ring,
         tc.tile_pool(name="flipped", bufs=2) as flipped,
-        tc.psum_pool(name="flip_banks", bufs=3) as flip_banks,
+        tc.psum_pool(name="flip_banks", bufs=LAG + 2) as flip_banks,
         tc.psum_pool(name="sum_banks", bufs=2) as sum_banks,
+        tc.psum_pool(name="idle_banks", bufs=1) as idle_banks,
     ):
         identity = held.tile([P, P], F32, name="identity")
         make_identity(nc, identity[:])
 
+        zeros = held.tile([P, T], BF16, name="zeros")
+        nc.vector.memset(zeros[:], 0.0)
+        idle_bank = idle_banks.tile([P, T], F32, name="idle_bank")
+        for w in range(WARM):
+            nc.tensor.matmul(idle_bank[:], zeros[:, 0:P], zeros[:], start=True, stop=True)
+
         offsets = held.tile([P, N // 16], U16, name="offsets")
         nc.sync.dma_start(offsets[:], offs)
+        bias_tile = held.tile([P, BLOCKS], F32, name="bias_tile")
+        with nc.allow_non_contiguous_dma(reason="512 single floats, one to a partition and block"):
+            nc.scalar.dma_start(bias_tile[:], bias.rearrange("(b p) one -> p (b one)", p=P))
         scale_tiles = [held.tile([P, S], F32, name=f"scales{b}") for b in range(BLOCKS)]
         code_tiles = [held.tile([P, N], F32, name=f"codes{b}") for b in range(BLOCKS)]
-        bias_tiles = [held.tile([P, 1], F32, name=f"bias{b}") for b in range(BLOCKS)]
+        centred_tiles = [held.tile([P, N], F32, name=f"centred{b}") for b in range(BLOCKS)]
         act_tile = held.tile([P, N // P, T], BF16, name="act_tile")
         for b in range(BLOCKS):
             rows = slice(b * P, (b + 1) * P)
@@ -44,19 +55,14 @@ def tile_autograd4bitquantlinear_kernel(tc, scales, wq, act, bias, offs, out):
             for r in range(PIECES):
                 cols = slice(r * PIECE, (r + 1) * PIECE)
                 nc.sync.dma_start(code_tiles[b][:, cols], wq[rows, cols])
+                nc.gpsimd.tensor_scalar(centred_tiles[b][:, cols], code_tiles[b][:, cols], -ZERO_POINT, 1.0, ADD, MULT)
                 if b == 0:
                     ks = slice(r * FLIPS, (r + 1) * FLIPS)
                     nc.sync.dma_start(act_tile[:, ks, :], act_rows[:, ks, :])
-            nc.sync.dma_start(bias_tiles[b][:], bias[rows, :])
 
-        centred_tiles = [held.tile([P, N], F32, name=f"centred{b}") for b in range(BLOCKS)]
         steps = [(b, r) for b in range(BLOCKS) for r in range(PIECES)]
         weights = {}
         sums = {}
-
-        def centre(b, r):
-            cols = slice(r * PIECE, (r + 1) * PIECE)
-            nc.scalar.activation(centred_tiles[b][:, cols], code_tiles[b][:, cols], COPY, bias=-ZERO_POINT)
 
         def dequantise_and_flip(b, r):
             cols = slice(r * PIECE, (r + 1) * PIECE)
@@ -85,15 +91,11 @@ def tile_autograd4bitquantlinear_kernel(tc, scales, wq, act, bias, offs, out):
                 )
             if r == PIECES - 1:
                 result = ring.tile([P, T], F32, name="result")
-                nc.scalar.activation(result[:], sums[b][:], IDENTITY, bias=bias_tiles[b][:])
+                nc.scalar.activation(result[:], sums[b][:], IDENTITY, bias=bias_tile[:, b : b + 1])
                 nc.sync.dma_start(out[b * P : (b + 1) * P, :], result[:])
 
-        for i in range(AHEAD):
-            centre(*steps[i])
-        for i in range(len(steps) + 1):
-            if i + AHEAD < len(steps):
-                centre(*steps[i + AHEAD])
+        for i in range(len(steps) + LAG):
             if i < len(steps):
                 dequantise_and_flip(*steps[i])
-            if i >= 1:
-                multiply(*steps[i - 1])
+            if i >= LAG:
+                multiply(*steps[i - LAG])

@@ -2,7 +2,7 @@ import concourse.mybir as mybir
 from concourse.masks import make_identity
 
 F32, BF16, U16 = mybir.dt.float32, mybir.dt.bfloat16, mybir.dt.uint16
-MULT, ADD = mybir.AluOpType.mult, mybir.AluOpType.add
+MULT = mybir.AluOpType.mult
 COPY = mybir.ActivationFunctionType.Copy
 IDENTITY = mybir.ActivationFunctionType.Identity
 
@@ -14,6 +14,7 @@ PIECE = S
 PIECES = N // PIECE
 FLIPS = PIECE // P
 WARM = 6
+AHEAD = 2
 LAG = 2
 
 FLOPS = 2 * C * N * T
@@ -55,7 +56,6 @@ def tile_autograd4bitquantlinear_kernel(tc, scales, wq, act, bias, offs, out):
             for r in range(PIECES):
                 cols = slice(r * PIECE, (r + 1) * PIECE)
                 nc.sync.dma_start(code_tiles[b][:, cols], wq[rows, cols])
-                nc.gpsimd.tensor_scalar(centred_tiles[b][:, cols], code_tiles[b][:, cols], -ZERO_POINT, 1.0, ADD, MULT)
                 if b == 0:
                     ks = slice(r * FLIPS, (r + 1) * FLIPS)
                     nc.sync.dma_start(act_tile[:, ks, :], act_rows[:, ks, :])
@@ -63,6 +63,10 @@ def tile_autograd4bitquantlinear_kernel(tc, scales, wq, act, bias, offs, out):
         steps = [(b, r) for b in range(BLOCKS) for r in range(PIECES)]
         weights = {}
         sums = {}
+
+        def centre(b, r):
+            cols = slice(r * PIECE, (r + 1) * PIECE)
+            nc.scalar.activation(centred_tiles[b][:, cols], code_tiles[b][:, cols], COPY, bias=-ZERO_POINT)
 
         def dequantise_and_flip(b, r):
             cols = slice(r * PIECE, (r + 1) * PIECE)
@@ -94,7 +98,11 @@ def tile_autograd4bitquantlinear_kernel(tc, scales, wq, act, bias, offs, out):
                 nc.scalar.activation(result[:], sums[b][:], IDENTITY, bias=bias_tile[:, b : b + 1])
                 nc.sync.dma_start(out[b * P : (b + 1) * P, :], result[:])
 
+        for i in range(AHEAD):
+            centre(*steps[i])
         for i in range(len(steps) + LAG):
+            if i + AHEAD < len(steps):
+                centre(*steps[i + AHEAD])
             if i < len(steps):
                 dequantise_and_flip(*steps[i])
             if i >= LAG:

@@ -27,19 +27,19 @@ def tile_autograd4bitquantlinear_kernel(tc, scales, wq, act, bias, offs, out):
     with (
         tc.tile_pool(name="held", bufs=1) as held,
         tc.tile_pool(name="ring", bufs=LAG + 2) as ring,
-        tc.tile_pool(name="flipped", bufs=2) as flipped,
-        tc.psum_pool(name="flip_banks", bufs=LAG + 2) as flip_banks,
-        tc.psum_pool(name="sum_banks", bufs=2) as sum_banks,
-        tc.psum_pool(name="idle_banks", bufs=1) as idle_banks,
+        tc.psum_pool(name="flip_banks", bufs=3) as flip_banks,
+        tc.psum_pool(name="held_banks", bufs=1) as held_banks,
     ):
         identity = held.tile([P, P], F32, name="identity")
         make_identity(nc, identity[:])
 
         zeros = held.tile([P, T], BF16, name="zeros")
         nc.vector.memset(zeros[:], 0.0)
-        idle_bank = idle_banks.tile([P, T], F32, name="idle_bank")
+        idle_bank = held_banks.tile([P, T], F32, name="idle_bank")
         for w in range(WARM):
             nc.tensor.matmul(idle_bank[:], zeros[:, 0:P], zeros[:], start=True, stop=True)
+
+        steps = [(r, b) for r in range(PIECES) for b in range(BLOCKS)]
 
         offsets = held.tile([P, N // 16], U16, name="offsets")
         nc.sync.dma_start(offsets[:], offs)
@@ -50,25 +50,24 @@ def tile_autograd4bitquantlinear_kernel(tc, scales, wq, act, bias, offs, out):
         code_tiles = [held.tile([P, N], F32, name=f"codes{b}") for b in range(BLOCKS)]
         centred_tiles = [held.tile([P, N], F32, name=f"centred{b}") for b in range(BLOCKS)]
         act_tile = held.tile([P, N // P, T], BF16, name="act_tile")
-        for b in range(BLOCKS):
+        for r, b in steps:
             rows = slice(b * P, (b + 1) * P)
-            nc.sync.dma_start(scale_tiles[b][:], scales[rows, :])
-            for r in range(PIECES):
-                cols = slice(r * PIECE, (r + 1) * PIECE)
-                nc.sync.dma_start(code_tiles[b][:, cols], wq[rows, cols])
-                if b == 0:
-                    ks = slice(r * FLIPS, (r + 1) * FLIPS)
-                    nc.sync.dma_start(act_tile[:, ks, :], act_rows[:, ks, :])
+            cols = slice(r * PIECE, (r + 1) * PIECE)
+            if r == 0:
+                nc.sync.dma_start(scale_tiles[b][:], scales[rows, :])
+            nc.sync.dma_start(code_tiles[b][:, cols], wq[rows, cols])
+            if b == 0:
+                ks = slice(r * FLIPS, (r + 1) * FLIPS)
+                nc.sync.dma_start(act_tile[:, ks, :], act_rows[:, ks, :])
 
-        steps = [(b, r) for b in range(BLOCKS) for r in range(PIECES)]
-        weights = {}
-        sums = {}
+        sums = [held_banks.tile([P, T], F32, name=f"sums{b}") for b in range(BLOCKS)]
+        flipped = {}
 
-        def centre(b, r):
+        def centre(r, b):
             cols = slice(r * PIECE, (r + 1) * PIECE)
             nc.scalar.activation(centred_tiles[b][:, cols], code_tiles[b][:, cols], COPY, bias=-ZERO_POINT)
 
-        def dequantise_and_flip(b, r):
+        def dequantise_and_flip(r, b):
             cols = slice(r * PIECE, (r + 1) * PIECE)
             picked = scale_tiles[b][:].indirect(offsets[:, r * (PIECE // 16) : (r + 1) * (PIECE // 16)])
             w_piece = ring.tile([P, PIECE], F32, name="w_piece")
@@ -77,25 +76,25 @@ def tile_autograd4bitquantlinear_kernel(tc, scales, wq, act, bias, offs, out):
             for f in range(FLIPS):
                 part = slice(f * P, (f + 1) * P)
                 nc.tensor.transpose(bank[:, part], w_piece[:, part], identity[:])
-            if r == 0:
-                weights[b] = flipped.tile([P, N], BF16, name="weights")
-            nc.scalar.activation(weights[b][:, cols], bank[:], COPY)
+            flipped[r, b] = ring.tile([P, PIECE], BF16, name="flipped")
+            nc.scalar.activation(flipped[r, b][:], bank[:], COPY)
 
-        def multiply(b, r):
-            if r == 0:
-                sums[b] = sum_banks.tile([P, T], F32, name="sums")
+        def multiply(r, b):
             for f in range(FLIPS):
                 k = r * FLIPS + f
                 nc.tensor.matmul(
                     sums[b][:],
-                    weights[b][:, k * P : (k + 1) * P],
+                    flipped[r, b][:, f * P : (f + 1) * P],
                     act_tile[:, k, :],
                     start=(k == 0),
                     stop=(k == N // P - 1),
                 )
             if r == PIECES - 1:
                 result = ring.tile([P, T], F32, name="result")
-                nc.scalar.activation(result[:], sums[b][:], IDENTITY, bias=bias_tile[:, b : b + 1])
+                if b % 2 == 0:
+                    nc.scalar.activation(result[:], sums[b][:], IDENTITY, bias=bias_tile[:, b : b + 1])
+                else:
+                    nc.vector.tensor_scalar_add(result[:], sums[b][:], bias_tile[:, b : b + 1])
                 nc.sync.dma_start(out[b * P : (b + 1) * P, :], result[:])
 
         for i in range(AHEAD):

@@ -65,7 +65,10 @@ def tile_autograd4bitquantlinear_kernel(tc, scales, wq, act, bias, offs, out):
 
         def centre(r, b):
             cols = slice(r * PIECE, (r + 1) * PIECE)
-            nc.scalar.activation(centred_tiles[b][:, cols], code_tiles[b][:, cols], COPY, bias=-ZERO_POINT)
+            if b % 2 == 0:
+                nc.vector.tensor_scalar_add(centred_tiles[b][:, cols], code_tiles[b][:, cols], -ZERO_POINT)
+            else:
+                nc.scalar.activation(centred_tiles[b][:, cols], code_tiles[b][:, cols], COPY, bias=-ZERO_POINT)
 
         def dequantise_and_flip(r, b):
             cols = slice(r * PIECE, (r + 1) * PIECE)

@@ -15,6 +15,7 @@ PIECES = N // PIECE
 FLIPS = PIECE // P
 WARM = 6
 AHEAD = 2
+RUN_AHEAD = 8
 LAG = 2
 
 FLOPS = 2 * C * N * T
@@ -27,6 +28,7 @@ def tile_autograd4bitquantlinear_kernel(tc, scales, wq, act, bias, offs, out):
     with (
         tc.tile_pool(name="held", bufs=1) as held,
         tc.tile_pool(name="ring", bufs=LAG + 2) as ring,
+        tc.tile_pool(name="products", bufs=RUN_AHEAD) as products,
         tc.psum_pool(name="flip_banks", bufs=3) as flip_banks,
         tc.psum_pool(name="held_banks", bufs=1) as held_banks,
     ):
@@ -56,7 +58,7 @@ def tile_autograd4bitquantlinear_kernel(tc, scales, wq, act, bias, offs, out):
             if r == 0:
                 nc.sync.dma_start(scale_tiles[b][:], scales[rows, :])
             nc.sync.dma_start(code_tiles[b][:, cols], wq[rows, cols])
-            if b == 0:
+            if b == BLOCKS - 1:
                 ks = slice(r * FLIPS, (r + 1) * FLIPS)
                 nc.sync.dma_start(act_tile[:, ks, :], act_rows[:, ks, :])
 
@@ -65,15 +67,12 @@ def tile_autograd4bitquantlinear_kernel(tc, scales, wq, act, bias, offs, out):
 
         def centre(r, b):
             cols = slice(r * PIECE, (r + 1) * PIECE)
-            if b % 2 == 0:
-                nc.vector.tensor_scalar_add(centred_tiles[b][:, cols], code_tiles[b][:, cols], -ZERO_POINT)
-            else:
-                nc.scalar.activation(centred_tiles[b][:, cols], code_tiles[b][:, cols], COPY, bias=-ZERO_POINT)
+            nc.scalar.activation(centred_tiles[b][:, cols], code_tiles[b][:, cols], COPY, bias=-ZERO_POINT)
 
         def dequantise_and_flip(r, b):
             cols = slice(r * PIECE, (r + 1) * PIECE)
             picked = scale_tiles[b][:].indirect(offsets[:, r * (PIECE // 16) : (r + 1) * (PIECE // 16)])
-            w_piece = ring.tile([P, PIECE], F32, name="w_piece")
+            w_piece = products.tile([P, PIECE], F32, name="w_piece")
             nc.vector.tensor_tensor(w_piece[:], picked, centred_tiles[b][:, cols], MULT)
             bank = flip_banks.tile([P, PIECE], F32, name="bank")
             for f in range(FLIPS):

@@ -45,9 +45,6 @@ def tile_autograd4bitquantlinear_kernel(tc, scales, wq, act, bias, offs, out):
 
         offsets = held.tile([P, N // 16], U16, name="offsets")
         nc.sync.dma_start(offsets[:], offs)
-        bias_tile = held.tile([P, BLOCKS], F32, name="bias_tile")
-        with nc.allow_non_contiguous_dma(reason="512 single floats, one to a partition and block"):
-            nc.scalar.dma_start(bias_tile[:], bias.rearrange("(b p) one -> p (b one)", p=P))
         scale_tiles = [held.tile([P, S], F32, name=f"scales{b}") for b in range(BLOCKS)]
         code_tiles = [held.tile([P, N], F32, name=f"codes{b}") for b in range(BLOCKS)]
         centred_tiles = [held.tile([P, N], F32, name=f"centred{b}") for b in range(BLOCKS)]
@@ -55,12 +52,15 @@ def tile_autograd4bitquantlinear_kernel(tc, scales, wq, act, bias, offs, out):
         for r, b in steps:
             rows = slice(b * P, (b + 1) * P)
             cols = slice(r * PIECE, (r + 1) * PIECE)
+            nc.sync.dma_start(code_tiles[b][:, cols], wq[rows, cols])
             if r == 0:
                 nc.sync.dma_start(scale_tiles[b][:], scales[rows, :])
-            nc.sync.dma_start(code_tiles[b][:, cols], wq[rows, cols])
             if b == BLOCKS - 1:
                 ks = slice(r * FLIPS, (r + 1) * FLIPS)
                 nc.sync.dma_start(act_tile[:, ks, :], act_rows[:, ks, :])
+        bias_tile = held.tile([P, BLOCKS], F32, name="bias_tile")
+        with nc.allow_non_contiguous_dma(reason="512 single floats, one to a partition and block"):
+            nc.sync.dma_start(bias_tile[:], bias.rearrange("(b p) one -> p (b one)", p=P))
 
         sums = [held_banks.tile([P, T], F32, name=f"sums{b}") for b in range(BLOCKS)]
         flipped = {}

@@ -29,6 +29,7 @@ def tile_autograd4bitquantlinear_kernel(tc, scales, wq, act, bias, offs, out):
         tc.tile_pool(name="held", bufs=1) as held,
         tc.tile_pool(name="ring", bufs=LAG + 2) as ring,
         tc.tile_pool(name="products", bufs=RUN_AHEAD) as products,
+        tc.tile_pool(name="results", bufs=BLOCKS + 1) as results,
         tc.psum_pool(name="flip_banks", bufs=3) as flip_banks,
         tc.psum_pool(name="held_banks", bufs=1) as held_banks,
     ):
@@ -37,11 +38,17 @@ def tile_autograd4bitquantlinear_kernel(tc, scales, wq, act, bias, offs, out):
 
         zeros = held.tile([P, T], BF16, name="zeros")
         nc.vector.memset(zeros[:], 0.0)
-        idle_bank = held_banks.tile([P, T], F32, name="idle_bank")
+        sums = [
+            [held_banks.tile([P, T // halves], F32, name=f"sums{b}_{h}") for h in range(halves)]
+            for b, halves in enumerate([1] * (BLOCKS - 1) + [2])
+        ]
         for w in range(WARM):
-            nc.tensor.matmul(idle_bank[:], zeros[:, 0:P], zeros[:], start=True, stop=True)
+            nc.tensor.matmul(sums[0][0][:], zeros[:, 0:P], zeros[:], start=True, stop=True)
 
-        steps = [(r, b) for r in range(PIECES) for b in range(BLOCKS)]
+        steps = [(r, b) for r in range(PIECES // 2) for b in range(BLOCKS)]
+        steps += [(r, b) for b in range(BLOCKS) for r in range(PIECES // 2, PIECES)]
+        last_step_of = {b: steps.index((PIECES - 1, b)) for b in range(BLOCKS)}
+        act_behind = {steps.index((r, 0)) + 3: r for r in range(PIECES)}
 
         offsets = held.tile([P, N // 16], U16, name="offsets")
         nc.sync.dma_start(offsets[:], offs)
@@ -49,20 +56,19 @@ def tile_autograd4bitquantlinear_kernel(tc, scales, wq, act, bias, offs, out):
         code_tiles = [held.tile([P, N], F32, name=f"codes{b}") for b in range(BLOCKS)]
         centred_tiles = [held.tile([P, N], F32, name=f"centred{b}") for b in range(BLOCKS)]
         act_tile = held.tile([P, N // P, T], BF16, name="act_tile")
-        for r, b in steps:
+        for i, (r, b) in enumerate(steps):
             rows = slice(b * P, (b + 1) * P)
             cols = slice(r * PIECE, (r + 1) * PIECE)
             nc.sync.dma_start(code_tiles[b][:, cols], wq[rows, cols])
             if r == 0:
                 nc.sync.dma_start(scale_tiles[b][:], scales[rows, :])
-            if b == BLOCKS - 1:
-                ks = slice(r * FLIPS, (r + 1) * FLIPS)
+            if i in act_behind:
+                ks = slice(act_behind[i] * FLIPS, (act_behind[i] + 1) * FLIPS)
                 nc.sync.dma_start(act_tile[:, ks, :], act_rows[:, ks, :])
         bias_tile = held.tile([P, BLOCKS], F32, name="bias_tile")
         with nc.allow_non_contiguous_dma(reason="512 single floats, one to a partition and block"):
             nc.sync.dma_start(bias_tile[:], bias.rearrange("(b p) one -> p (b one)", p=P))
 
-        sums = [held_banks.tile([P, T], F32, name=f"sums{b}") for b in range(BLOCKS)]
         flipped = {}
 
         def centre(r, b):
@@ -82,22 +88,27 @@ def tile_autograd4bitquantlinear_kernel(tc, scales, wq, act, bias, offs, out):
             nc.scalar.activation(flipped[r, b][:], bank[:], COPY)
 
         def multiply(r, b):
-            for f in range(FLIPS):
-                k = r * FLIPS + f
-                nc.tensor.matmul(
-                    sums[b][:],
-                    flipped[r, b][:, f * P : (f + 1) * P],
-                    act_tile[:, k, :],
-                    start=(k == 0),
-                    stop=(k == N // P - 1),
-                )
-            if r == PIECES - 1:
-                result = ring.tile([P, T], F32, name="result")
-                if b % 2 == 0:
-                    nc.scalar.activation(result[:], sums[b][:], IDENTITY, bias=bias_tile[:, b : b + 1])
+            width = T // len(sums[b])
+            for h, bank in enumerate(sums[b]):
+                for f in range(FLIPS):
+                    k = r * FLIPS + f
+                    nc.tensor.matmul(
+                        bank[:],
+                        flipped[r, b][:, f * P : (f + 1) * P],
+                        act_tile[:, k, h * width : (h + 1) * width],
+                        start=(k == 0),
+                        stop=(k == N // P - 1),
+                    )
+
+        def finish(b, engine):
+            width = T // len(sums[b])
+            for h, bank in enumerate(sums[b]):
+                result = results.tile([P, width], F32, name="result")
+                if engine == "scalar":
+                    nc.scalar.activation(result[:], bank[:], IDENTITY, bias=bias_tile[:, b : b + 1])
                 else:
-                    nc.vector.tensor_scalar_add(result[:], sums[b][:], bias_tile[:, b : b + 1])
-                nc.sync.dma_start(out[b * P : (b + 1) * P, :], result[:])
+                    nc.vector.tensor_scalar_add(result[:], bank[:], bias_tile[:, b : b + 1])
+                nc.sync.dma_start(out[b * P : (b + 1) * P, h * width : (h + 1) * width], result[:])
 
         for i in range(AHEAD):
             centre(*steps[i])
@@ -107,4 +118,7 @@ def tile_autograd4bitquantlinear_kernel(tc, scales, wq, act, bias, offs, out):
             if i < len(steps):
                 dequantise_and_flip(*steps[i])
             if i >= LAG:
-                multiply(*steps[i - LAG])
+                r, b = steps[i - LAG]
+                multiply(r, b)
+                if i - LAG == last_step_of[b]:
+                    finish(b, "vector" if b == BLOCKS - 1 else "scalar")

@@ -24,6 +24,9 @@ FLOPS = 2 * C * N * T
 def tile_autograd4bitquantlinear_kernel(tc, scales, wq, act, bias, offs, out):
     nc = tc.nc
     act_rows = act.rearrange("(k p) t -> p k t", p=P)
+    scales_blocks = scales.rearrange("(p b) s -> b p s", b=BLOCKS)
+    wq_blocks = wq.rearrange("(p b) n -> b p n", b=BLOCKS)
+    out_blocks = out.rearrange("(p b) t -> b p t", b=BLOCKS)
 
     with (
         tc.tile_pool(name="held", bufs=1) as held,
@@ -56,18 +59,16 @@ def tile_autograd4bitquantlinear_kernel(tc, scales, wq, act, bias, offs, out):
         code_tiles = [held.tile([P, N], F32, name=f"codes{b}") for b in range(BLOCKS)]
         centred_tiles = [held.tile([P, N], F32, name=f"centred{b}") for b in range(BLOCKS)]
         act_tile = held.tile([P, N // P, T], BF16, name="act_tile")
+        bias_tile = held.tile([P, BLOCKS], F32, name="bias_tile")
         for i, (r, b) in enumerate(steps):
-            rows = slice(b * P, (b + 1) * P)
             cols = slice(r * PIECE, (r + 1) * PIECE)
-            nc.sync.dma_start(code_tiles[b][:, cols], wq[rows, cols])
+            nc.sync.dma_start(code_tiles[b][:, cols], wq_blocks[b][:, cols])
             if r == 0:
-                nc.sync.dma_start(scale_tiles[b][:], scales[rows, :])
+                nc.sync.dma_start(scale_tiles[b][:], scales_blocks[b])
             if i in act_behind:
                 ks = slice(act_behind[i] * FLIPS, (act_behind[i] + 1) * FLIPS)
                 nc.sync.dma_start(act_tile[:, ks, :], act_rows[:, ks, :])
-        bias_tile = held.tile([P, BLOCKS], F32, name="bias_tile")
-        with nc.allow_non_contiguous_dma(reason="512 single floats, one to a partition and block"):
-            nc.sync.dma_start(bias_tile[:], bias.rearrange("(b p) one -> p (b one)", p=P))
+        nc.sync.dma_start(bias_tile[:], bias.rearrange("(p b) one -> p (b one)", b=BLOCKS))
 
         flipped = {}
 
@@ -108,7 +109,7 @@ def tile_autograd4bitquantlinear_kernel(tc, scales, wq, act, bias, offs, out):
                     nc.scalar.activation(result[:], bank[:], IDENTITY, bias=bias_tile[:, b : b + 1])
                 else:
                     nc.vector.tensor_scalar_add(result[:], bank[:], bias_tile[:, b : b + 1])
-                nc.sync.dma_start(out[b * P : (b + 1) * P, h * width : (h + 1) * width], result[:])
+                nc.sync.dma_start(out_blocks[b][:, h * width : (h + 1) * width], result[:])
 
         for i in range(AHEAD):
             centre(*steps[i])

@@ -13,7 +13,7 @@ BLOCKS = C // P
 PIECE = S
 PIECES = N // PIECE
 FLIPS = PIECE // P
-WARM = 6
+WARM = 10
 AHEAD = 2
 RUN_AHEAD = 8
 LAG = 2

@@ -51,7 +51,7 @@ def tile_autograd4bitquantlinear_kernel(tc, scales, wq, act, bias, offs, out):
         steps = [(r, b) for r in range(PIECES // 2) for b in range(BLOCKS)]
         steps += [(r, b) for b in range(BLOCKS) for r in range(PIECES // 2, PIECES)]
         last_step_of = {b: steps.index((PIECES - 1, b)) for b in range(BLOCKS)}
-        act_behind = {steps.index((r, 0)) + 3: r for r in range(PIECES)}
+        act_behind = {steps.index((r, 0)) + 4: r for r in range(PIECES)}
 
         offsets = held.tile([P, N // 16], U16, name="offsets")
         nc.sync.dma_start(offsets[:], offs)

@@ -51,7 +51,7 @@ def tile_autograd4bitquantlinear_kernel(tc, scales, wq, act, bias, offs, out):
         steps = [(r, b) for r in range(PIECES // 2) for b in range(BLOCKS)]
         steps += [(r, b) for b in range(BLOCKS) for r in range(PIECES // 2, PIECES)]
         last_step_of = {b: steps.index((PIECES - 1, b)) for b in range(BLOCKS)}
-        act_behind = {steps.index((r, 0)) + 4: r for r in range(PIECES)}
+        act_behind = {steps.index((r, 0)) + (5 if r == 0 else 4): r for r in range(PIECES)}
 
         offsets = held.tile([P, N // 16], U16, name="offsets")
         nc.sync.dma_start(offsets[:], offs)

@@ -13,7 +13,7 @@ BLOCKS = C // P
 PIECE = S
 PIECES = N // PIECE
 FLIPS = PIECE // P
-WARM = 10
+WARM = 12
 AHEAD = 2
 RUN_AHEAD = 8
 LAG = 2

@@ -70,6 +70,7 @@ def tile_autograd4bitquantlinear_kernel(tc, scales, wq, act, bias, offs, out):
                 nc.sync.dma_start(act_tile[:, ks, :], act_rows[:, ks, :])
         nc.sync.dma_start(bias_tile[:], bias.rearrange("(p b) one -> p (b one)", b=BLOCKS))
 
+        complete = []
         flipped = {}
 
         def centre(r, b):
@@ -122,4 +123,8 @@ def tile_autograd4bitquantlinear_kernel(tc, scales, wq, act, bias, offs, out):
                 r, b = steps[i - LAG]
                 multiply(r, b)
                 if i - LAG == last_step_of[b]:
-                    finish(b, "vector" if b == BLOCKS - 1 else "scalar")
+                    complete.append(b)
+            if i >= len(steps) - 1:
+                for b in complete:
+                    finish(b, "scalar" if b == BLOCKS - 2 else "vector")
+                complete.clear()

@@ -13,7 +13,7 @@ BLOCKS = C // P
 PIECE = S
 PIECES = N // PIECE
 FLIPS = PIECE // P
-WARM = 12
+WARM = 8
 AHEAD = 2
 RUN_AHEAD = 8
 LAG = 2

import concourse.mybir as mybir
from concourse.masks import make_identity

F32, BF16, U16 = mybir.dt.float32, mybir.dt.bfloat16, mybir.dt.uint16
MULT = mybir.AluOpType.mult
COPY = mybir.ActivationFunctionType.Copy
IDENTITY = mybir.ActivationFunctionType.Identity

P = 128
C, S, N, T = 512, 256, 1024, 512
ZERO_POINT = 8.0
BLOCKS = C // P
PIECE = S
PIECES = N // PIECE
FLIPS = PIECE // P
WARM = 8
AHEAD = 2
RUN_AHEAD = 8
LAG = 2

FLOPS = 2 * C * N * T


def tile_autograd4bitquantlinear_kernel(tc, scales, wq, act, bias, offs, out):
    nc = tc.nc
    act_rows = act.rearrange("(k p) t -> p k t", p=P)
    scales_blocks = scales.rearrange("(p b) s -> b p s", b=BLOCKS)
    wq_blocks = wq.rearrange("(p b) n -> b p n", b=BLOCKS)
    out_blocks = out.rearrange("(p b) t -> b p t", b=BLOCKS)

    with (
        tc.tile_pool(name="held", bufs=1) as held,
        tc.tile_pool(name="ring", bufs=LAG + 2) as ring,
        tc.tile_pool(name="products", bufs=RUN_AHEAD) as products,
        tc.tile_pool(name="results", bufs=BLOCKS + 1) as results,
        tc.psum_pool(name="flip_banks", bufs=3) as flip_banks,
        tc.psum_pool(name="held_banks", bufs=1) as held_banks,
    ):
        identity = held.tile([P, P], F32, name="identity")
        make_identity(nc, identity[:])

        zeros = held.tile([P, T], BF16, name="zeros")
        nc.vector.memset(zeros[:], 0.0)
        sums = [
            [held_banks.tile([P, T // halves], F32, name=f"sums{b}_{h}") for h in range(halves)]
            for b, halves in enumerate([1] * (BLOCKS - 1) + [2])
        ]
        for w in range(WARM):
            nc.tensor.matmul(sums[0][0][:], zeros[:, 0:P], zeros[:], start=True, stop=True)

        steps = [(r, b) for r in range(PIECES // 2) for b in range(BLOCKS)]
        steps += [(r, b) for b in range(BLOCKS) for r in range(PIECES // 2, PIECES)]
        last_step_of = {b: steps.index((PIECES - 1, b)) for b in range(BLOCKS)}
        act_behind = {steps.index((r, 0)) + (5 if r == 0 else 4): r for r in range(PIECES)}

        offsets = held.tile([P, N // 16], U16, name="offsets")
        nc.sync.dma_start(offsets[:], offs)
        scale_tiles = [held.tile([P, S], F32, name=f"scales{b}") for b in range(BLOCKS)]
        code_tiles = [held.tile([P, N], F32, name=f"codes{b}") for b in range(BLOCKS)]
        centred_tiles = [held.tile([P, N], F32, name=f"centred{b}") for b in range(BLOCKS)]
        act_tile = held.tile([P, N // P, T], BF16, name="act_tile")
        bias_tile = held.tile([P, BLOCKS], F32, name="bias_tile")
        for i, (r, b) in enumerate(steps):
            cols = slice(r * PIECE, (r + 1) * PIECE)
            nc.sync.dma_start(code_tiles[b][:, cols], wq_blocks[b][:, cols])
            if r == 0:
                nc.sync.dma_start(scale_tiles[b][:], scales_blocks[b])
            if i in act_behind:
                ks = slice(act_behind[i] * FLIPS, (act_behind[i] + 1) * FLIPS)
                nc.sync.dma_start(act_tile[:, ks, :], act_rows[:, ks, :])
        nc.sync.dma_start(bias_tile[:], bias.rearrange("(p b) one -> p (b one)", b=BLOCKS))

        complete = []
        flipped = {}

        def centre(r, b):
            cols = slice(r * PIECE, (r + 1) * PIECE)
            nc.scalar.activation(centred_tiles[b][:, cols], code_tiles[b][:, cols], COPY, bias=-ZERO_POINT)

        def dequantise_and_flip(r, b):
            cols = slice(r * PIECE, (r + 1) * PIECE)
            picked = scale_tiles[b][:].indirect(offsets[:, r * (PIECE // 16) : (r + 1) * (PIECE // 16)])
            w_piece = products.tile([P, PIECE], F32, name="w_piece")
            nc.vector.tensor_tensor(w_piece[:], picked, centred_tiles[b][:, cols], MULT)
            bank = flip_banks.tile([P, PIECE], F32, name="bank")
            for f in range(FLIPS):
                part = slice(f * P, (f + 1) * P)
                nc.tensor.transpose(bank[:, part], w_piece[:, part], identity[:])
            flipped[r, b] = ring.tile([P, PIECE], BF16, name="flipped")
            nc.scalar.activation(flipped[r, b][:], bank[:], COPY)

        def multiply(r, b):
            width = T // len(sums[b])
            for h, bank in enumerate(sums[b]):
                for f in range(FLIPS):
                    k = r * FLIPS + f
                    nc.tensor.matmul(
                        bank[:],
                        flipped[r, b][:, f * P : (f + 1) * P],
                        act_tile[:, k, h * width : (h + 1) * width],
                        start=(k == 0),
                        stop=(k == N // P - 1),
                    )

        def finish(b, engine):
            width = T // len(sums[b])
            for h, bank in enumerate(sums[b]):
                result = results.tile([P, width], F32, name="result")
                if engine == "scalar":
                    nc.scalar.activation(result[:], bank[:], IDENTITY, bias=bias_tile[:, b : b + 1])
                else:
                    nc.vector.tensor_scalar_add(result[:], bank[:], bias_tile[:, b : b + 1])
                nc.sync.dma_start(out_blocks[b][:, h * width : (h + 1) * width], result[:])

        for i in range(AHEAD):
            centre(*steps[i])
        for i in range(len(steps) + LAG):
            if i + AHEAD < len(steps):
                centre(*steps[i + AHEAD])
            if i < len(steps):
                dequantise_and_flip(*steps[i])
            if i >= LAG:
                r, b = steps[i - LAG]
                multiply(r, b)
                if i - LAG == last_step_of[b]:
                    complete.append(b)
            if i >= len(steps) - 1:
                for b in complete:
                    finish(b, "scalar" if b == BLOCKS - 2 else "vector")
                complete.clear()
